import numpy as np
import ml_dtypes


def mxq(x, axis, fmt="e4m3"):
    dtype, down = {"e4m3": (ml_dtypes.float8_e4m3fn, 7), "e5m2": (ml_dtypes.float8_e5m2, 14)}[fmt]
    v = np.moveaxis(np.asarray(x, np.float32).astype(ml_dtypes.bfloat16).astype(np.float64), axis, -1)
    blocks = v.reshape(v.shape[:-1] + (-1, 32))
    amax = np.abs(blocks).max(-1, keepdims=True)
    byte = np.maximum(np.where(amax > 0, np.frexp(amax)[1] - 1 + 127, 0) - down, 1)
    scale = np.exp2(byte - 127.0)
    codes = (blocks / scale).astype(np.float32).astype(dtype).astype(np.float64)
    return np.moveaxis((codes * scale).reshape(v.shape), -1, axis)


WIDE = False


def mx_kscale(k):
    if not WIDE:
        return np.ones(k)
    levels = np.array([10, -10, 5, -5, 0])
    a = np.random.permutation(np.resize(levels, k // 512 * 4)).reshape(k // 512, 4)
    idx = np.arange(k)
    return np.exp2(a[idx // 512, idx % 128 // 32])


BF16 = ml_dtypes.bfloat16


def bf(x):
    return np.asarray(x, np.float32).astype(BF16)


def f64(x):
    return np.asarray(x).astype(np.float64)


E2M1 = np.array([0.0, 0.5, 1.0, 1.5, 2.0, 3.0, 4.0, 6.0, -0.0, -0.5, -1.0, -1.5, -2.0, -3.0, -4.0, -6.0])


def pack_weight(w, fmt):
    k, n = w.shape
    w = f64(bf(w)).reshape(k // 32, 32, n)
    amax = np.abs(w).max(1)
    if fmt == "e4m3":
        byte = np.frexp(amax)[1] - 1 + 127 - 7
    else:
        mant, ex = np.frexp(amax / 6.0)
        byte = np.where(mant > 0.5, ex, ex - 1) + 127
    byte = np.clip(np.where(amax > 0, byte, 1), 1, 254)
    scaled = (w * np.exp2(127.0 - byte)[:, None, :]).reshape(k, n).astype(np.float32)
    by_word = np.ascontiguousarray(scaled.reshape(k // 512, 128, 4, n).transpose(0, 1, 3, 2))
    if fmt == "e4m3":
        words = by_word.astype(ml_dtypes.float8_e4m3fn).view(np.uint8)
    else:
        c = by_word.astype(ml_dtypes.float4_e2m1fn).view(np.uint8) & 0xF
        words = c[..., 0::2] | (c[..., 1::2] << 4)
    return np.ascontiguousarray(words), np.ascontiguousarray(byte.astype(np.uint8).reshape(k // 512, 16, n))


def unpack_weight(words, scales, fmt):
    g, p, n, _ = words.shape
    if fmt == "e4m3":
        vals = np.ascontiguousarray(words).view(ml_dtypes.float8_e4m3fn).astype(np.float64)
    else:
        nib = np.empty((g, p, n, 4), np.uint8)
        nib[..., 0::2] = words & 0xF
        nib[..., 1::2] = words >> 4
        vals = E2M1[nib]
    vals = vals * np.repeat(np.exp2(scales.astype(np.float64) - 127.0), 8, axis=1)[..., None]
    return vals.transpose(0, 1, 3, 2).reshape(g * 512, n)


B, S, D, H, HD, M, G = 1, 128, 8192, 8, 128, 1280, 3
EPS = 1e-6
HH = H * HD
FMT = "e4m3"


def silu(v):
    return v / (1.0 + np.exp(-v))


def rmsnorm(x, gain):
    var = np.mean(np.square(x), axis=-1, keepdims=True)
    return x * (1.0 / np.sqrt(var + EPS)) * gain


def setup_inputs():
    s, t = mx_kscale(HH), mx_kscale(D)
    attn = bf(0.3 * np.random.standard_normal((B, S, HH)) * s)
    x = bf(np.random.standard_normal((B, S, D)))
    w_o_words, w_o_scales = pack_weight(np.random.standard_normal((HH, D)) * 2.0 / np.sqrt(HH) / s[:, None], FMT)
    rms2_scale = bf((1.0 + 0.1 * np.random.standard_normal(D)) * t)
    w_gate_words, w_gate_scales = pack_weight(np.random.standard_normal((D, M)) / np.sqrt(D) / t[:, None], FMT)
    w_up_words, w_up_scales = pack_weight(np.random.standard_normal((D, M)) / np.sqrt(D) / t[:, None], FMT)
    return {"attn": attn,
            "x": x,
            "w_o_words": w_o_words,
            "w_o_scales": w_o_scales,
            "rms2_scale": rms2_scale,
            "w_gate_words": w_gate_words,
            "w_gate_scales": w_gate_scales,
            "w_up_words": w_up_words,
            "w_up_scales": w_up_scales}


def reference(attn, x, w_o_words, w_o_scales, rms2_scale, w_gate_words, w_gate_scales, w_up_words, w_up_scales):
    x_mid = f64(x) + (mxq(f64(attn), 2, "e4m3") @ unpack_weight(w_o_words, w_o_scales, FMT))
    hq = mxq(rmsnorm(x_mid, f64(rms2_scale)), 2, "e4m3")
    g = silu(hq @ unpack_weight(w_gate_words, w_gate_scales, FMT)) * (hq @ unpack_weight(w_up_words, w_up_scales, FMT))
    return x_mid, g

@@ -1,0 +1,271 @@
+from contextlib import ExitStack
+
+import concourse.mybir as mybir
+from concourse.masks import make_identity
+
+F32 = mybir.dt.float32
+BF16 = mybir.dt.bfloat16
+I32 = mybir.dt.int32
+U32 = mybir.dt.uint32
+U8 = mybir.dt.uint8
+FP8X4 = mybir.dt.float8_e4m3fn_x4
+ALU = mybir.AluOpType
+ACT = mybir.ActivationFunctionType
+AXIS = mybir.AxisListType
+
+P = 128
+PACK = 4
+K_PASS = P * PACK
+BANK = 512
+QUADRANTS = 4
+
+HH = 1024
+D = 8192
+M = 1280
+EPS = 1e-6
+
+O_GROUPS = HH // K_PASS
+H_GROUPS = D // K_PASS
+O_CHUNK = 2048
+O_CHUNKS = D // O_CHUNK
+ROUND_GROUPS = 4
+ROUNDS = H_GROUPS // ROUND_GROUPS
+SHARED = 4
+RING = 7
+M_BLOCKS = ((0, 512), (512, 512), (1024, 256))
+
+FLOPS = 2 * P * (HH * D + D * 2 * M)
+
+
+def turn(nc, psum, stage, ident, sorted_rows, groups):
+    grouped = stage.tile([P, groups, P, PACK], BF16, align_bytes=64)
+    for pair in range(groups // 2):
+        turned = psum.tile([P, 2, PACK, P], BF16)
+        for half in range(2):
+            for t in range(PACK):
+                nc.tensor.transpose(turned[:, half, t, :], sorted_rows[:, t, 2 * pair + half, :], ident[:])
+        nc.scalar.copy(
+            out=grouped[:, 2 * pair : 2 * pair + 2, :, :],
+            in_=turned[:].rearrange("p g t r -> p g r t"),
+        )
+    return grouped
+
+
+def quantise(nc, grouped, codes, scales):
+    nc.vector.quantize_mx(
+        out=codes.bitcast(FP8X4),
+        scales=scales,
+        in_=grouped[:].rearrange("p g r t -> p (g r t)"),
+    )
+
+
+def tile_transformerblocktpu_pb_k_kernel(
+    tc,
+    attn,
+    x,
+    w_o_words,
+    w_o_scales,
+    rms2_scale,
+    w_gate_words,
+    w_gate_scales,
+    w_up_words,
+    w_up_scales,
+    out_0,
+    out_1,
+):
+    nc = tc.nc
+    attn_rows = attn.rearrange("b s k -> (b s) k")
+    x_rows = x.rearrange("b s d -> (b s) d")
+    x_mid_rows = out_0.rearrange("b s d -> (b s) d")
+    g_rows = out_1.rearrange("b s m -> (b s) m")
+    gu_words = (w_gate_words, w_up_words)
+    gu_scales = (w_gate_scales, w_up_scales)
+
+    with ExitStack() as ctx:
+        ctx.enter_context(tc.manual_schedule())
+        keep = ctx.enter_context(tc.tile_pool(name="keep", bufs=1))
+        ring = ctx.enter_context(tc.tile_pool(name="ring", bufs=RING))
+
+        x_mid = keep.tile([P, D], F32)
+        gain_all = keep.tile([P, D], BF16)
+        ident = keep.tile([P, P], BF16)
+        planes_o = keep.tile([P, D], U8, align_bytes=64)
+        planes_gu = keep.tile([P, 2, H_GROUPS // SHARED, M], U8, align_bytes=64)
+        sumsq = keep.tile([P, D // BANK], F32)
+        total = keep.tile([P, 1], F32)
+        mean_eps = keep.tile([P, 1], F32)
+        neg_half = keep.tile([P, 1], F32)
+        rstd = keep.tile([P, 1], F32)
+
+        nc.vector.memset(planes_o[:].bitcast(I32), 0)
+        nc.vector.memset(planes_gu[:].rearrange("p w j m -> p (w j m)").bitcast(I32), 0)
+        make_identity(nc, ident[:])
+        nc.gpsimd.memset(neg_half[:], -0.5)
+
+        def load_planes_gu(w, j, quadrant):
+            nc.sync.dma_start(
+                out=planes_gu[32 * quadrant : 32 * quadrant + 4 * SHARED, w, j, :].bitcast(I32),
+                in_=gu_scales[w][SHARED * j : SHARED * (j + 1), 4 * quadrant : 4 * quadrant + 4, :].bitcast(I32),
+            )
+
+        def load_group(g):
+            pair = ring.tile([P, 2, M], U32, align_bytes=64)
+            for w in range(2):
+                nc.sync.dma_start(
+                    out=pair[:, w, :].bitcast(I32),
+                    in_=gu_words[w][g].rearrange("p n t -> p (n t)").bitcast(I32),
+                )
+                if g // SHARED + 1 < H_GROUPS // SHARED:
+                    load_planes_gu(w, g // SHARED + 1, g % QUADRANTS)
+            return pair
+
+        with tc.tile_pool(name="stage1", bufs=1) as stage1, tc.tile_pool(name="junk", bufs=4) as junk_pool:
+            attn_sb = stage1.tile([P, HH], BF16)
+            nc.sync.dma_start(out=attn_sb[:], in_=attn_rows)
+            for quadrant in range(QUADRANTS):
+                nc.sync.dma_start(
+                    out=planes_o[32 * quadrant : 32 * quadrant + 4 * O_GROUPS, :].bitcast(I32),
+                    in_=w_o_scales[:, 4 * quadrant : 4 * quadrant + 4, :].bitcast(I32),
+                )
+            gain_rows = stage1.tile([P, K_PASS], BF16)
+            nc.vector.memset(gain_rows[:], 0.0)
+            nc.sync.dma_start(out=gain_rows[0:H_GROUPS, :], in_=rms2_scale.rearrange("(g n) -> g n", n=K_PASS))
+            x_sb = stage1.tile([P, D], BF16)
+            nc.sync.dma_start(out=x_sb[:], in_=x_rows)
+            o_words = []
+            for c in range(O_CHUNKS):
+                chunk = stage1.tile([P, O_GROUPS, O_CHUNK], U32, name="o_words%d" % c, align_bytes=64)
+                nc.sync.dma_start(
+                    out=chunk[:].bitcast(I32),
+                    in_=w_o_words[:, :, c * O_CHUNK : (c + 1) * O_CHUNK, :]
+                    .rearrange("g p n t -> p g (n t)")
+                    .bitcast(I32),
+                )
+                o_words.append(chunk)
+                for w in range(2):
+                    load_planes_gu(w, 0, c)
+            gu_tiles = {}
+            for g in range(RING):
+                gu_tiles[g] = load_group(g)
+
+            with tc.psum_pool(name="psum_turn1", bufs=1) as psum_turn1, tc.psum_pool(
+                name="psum_spread", bufs=2
+            ) as psum_spread, tc.psum_pool(name="psum_o", bufs=4) as psum_o:
+                attn_sorted = stage1.tile([P, PACK, O_GROUPS, P], BF16)
+                nc.vector.tensor_copy(
+                    out=attn_sorted[:], in_=attn_sb[:].rearrange("s (g p t) -> s t g p", p=P, t=PACK)
+                )
+                attn_grouped = turn(nc, psum_turn1, stage1, ident, attn_sorted, O_GROUPS)
+                attn_codes = stage1.tile([P, O_GROUPS * P], U32, align_bytes=64)
+                attn_scales = stage1.tile([P, O_GROUPS * P], U8, align_bytes=64)
+                quantise(nc, attn_grouped, attn_codes[:], attn_scales[:])
+
+                for pair in range(H_GROUPS // 2):
+                    spread = psum_spread.tile([P, 2, K_PASS], BF16)
+                    for half in range(2):
+                        g = 2 * pair + half
+                        nc.tensor.matmul(
+                            out=spread[:, half, :],
+                            lhsT=ident[:, g : g + 1].to_broadcast([P, P]),
+                            rhs=gain_rows[:],
+                            start=True,
+                            stop=True,
+                        )
+                    nc.scalar.copy(
+                        out=gain_all[:, 2 * pair * K_PASS : 2 * (pair + 1) * K_PASS],
+                        in_=spread[:].rearrange("p h n -> p (h n)"),
+                    )
+
+                for c in range(O_CHUNKS):
+                    for b in range(O_CHUNK // BANK):
+                        cols = slice(b * BANK, (b + 1) * BANK)
+                        d_cols = slice(c * O_CHUNK + b * BANK, c * O_CHUNK + (b + 1) * BANK)
+                        acc = psum_o.tile([P, BANK], F32)
+                        for g in range(O_GROUPS):
+                            nc.tensor.matmul_mx(
+                                out=acc[:],
+                                lhsT=attn_codes[:, g * P : (g + 1) * P].bitcast(FP8X4),
+                                lhsT_scale=attn_scales[:, g * P : (g + 1) * P],
+                                rhs=o_words[c][:, g, cols].bitcast(FP8X4),
+                                rhs_scale=planes_o[4 * g : P, d_cols],
+                                start=(g == 0),
+                                stop=(g == O_GROUPS - 1),
+                            )
+                        nc.vector.tensor_tensor(out=x_mid[:, d_cols], in0=acc[:], in1=x_sb[:, d_cols], op=ALU.add)
+                        junk = junk_pool.tile([P, BANK], BF16)
+                        bank = c * (O_CHUNK // BANK) + b
+                        nc.scalar.activation(
+                            out=junk[:], in_=x_mid[:, d_cols], func=ACT.Square, accum_out=sumsq[:, bank : bank + 1]
+                        )
+
+        nc.vector.tensor_reduce(out=total[:], in_=sumsq[:], axis=AXIS.X, op=ALU.add)
+        nc.vector.tensor_scalar(
+            out=mean_eps[:], in0=total[:], scalar1=1.0 / D, scalar2=EPS, op0=ALU.mult, op1=ALU.add
+        )
+        nc.gpsimd.tensor_tensor(out=rstd[:], in0=mean_eps[:], in1=neg_half[:], op=ALU.pow)
+
+        stage2 = ctx.enter_context(tc.tile_pool(name="stage2", bufs=2))
+        last = ctx.enter_context(tc.tile_pool(name="last", bufs=1))
+        psum_turn2 = ctx.enter_context(tc.psum_pool(name="psum_turn2", bufs=2))
+        psum_gu = ctx.enter_context(tc.psum_pool(name="psum_gu", bufs=1))
+
+        h_codes = last.tile([P, H_GROUPS * P], U32, align_bytes=64)
+        h_scales = last.tile([P, H_GROUPS * P], U8, align_bytes=64)
+        acc_gu = [
+            [psum_gu.tile([P, width], F32, name="acc%d_%d" % (w, first)) for first, width in M_BLOCKS]
+            for w in range(2)
+        ]
+
+        def normalise(r):
+            h_sorted = stage2.tile([P, PACK, ROUND_GROUPS, P], BF16)
+            k_cols = slice(r * ROUND_GROUPS * K_PASS, (r + 1) * ROUND_GROUPS * K_PASS)
+            x_view = x_mid[:, k_cols].rearrange("s (g p t) -> s t g p", p=P, t=PACK)
+            gain_view = gain_all[:, k_cols].rearrange("s (g p t) -> s t g p", p=P, t=PACK)
+            for t in range(PACK):
+                nc.vector.scalar_tensor_tensor(
+                    out=h_sorted[:, t, :, :],
+                    in0=x_view[:, t],
+                    scalar=rstd[:, 0:1],
+                    in1=gain_view[:, t],
+                    op0=ALU.mult,
+                    op1=ALU.mult,
+                )
+            return h_sorted
+
+        def multiply(g):
+            for w in range(2):
+                for blk, (first, width) in enumerate(M_BLOCKS):
+                    nc.tensor.matmul_mx(
+                        out=acc_gu[w][blk][:],
+                        lhsT=h_codes[:, g * P : (g + 1) * P].bitcast(FP8X4),
+                        lhsT_scale=h_scales[:, g * P : (g + 1) * P],
+                        rhs=gu_tiles[g][:, w, first : first + width].bitcast(FP8X4),
+                        rhs_scale=planes_gu[4 * (g % SHARED) : P, w, g // SHARED, first : first + width],
+                        start=(g == 0),
+                        stop=(g == H_GROUPS - 1),
+                    )
+
+        h_grouped = {}
+        for r in range(ROUNDS + 1):
+            if r < ROUNDS:
+                h_grouped[r] = turn(nc, psum_turn2, stage2, ident, normalise(r), ROUND_GROUPS)
+            if r > 0:
+                done = r - 1
+                word_cols = slice(done * ROUND_GROUPS * P, (done + 1) * ROUND_GROUPS * P)
+                quantise(nc, h_grouped[done], h_codes[:, word_cols], h_scales[:, word_cols])
+                for g in range(done * ROUND_GROUPS, (done + 1) * ROUND_GROUPS):
+                    multiply(g)
+                    if g + RING < H_GROUPS:
+                        gu_tiles[g + RING] = load_group(g + RING)
+
+        for c in range(O_CHUNKS):
+            d_cols = slice(c * O_CHUNK, (c + 1) * O_CHUNK)
+            nc.sync.dma_start(out=x_mid_rows[:, d_cols], in_=x_mid[:, d_cols])
+
+        gate_act = last.tile([P, M], F32)
+        g_sb = last.tile([P, M], F32)
+        for blk, (first, width) in enumerate(M_BLOCKS):
+            m_cols = slice(first, first + width)
+            nc.scalar.activation(out=gate_act[:, m_cols], in_=acc_gu[0][blk][:], func=ACT.Silu)
+            nc.vector.tensor_tensor(out=g_sb[:, m_cols], in0=acc_gu[1][blk][:], in1=gate_act[:, m_cols], op=ALU.mult)
+        nc.sync.dma_start(out=g_rows, in_=g_sb[:])

@@ -94,19 +94,20 @@ def tile_transformerblocktpu_pb_k_kernel(
         sumsq = keep.tile([P, D // BANK], F32)
         total = keep.tile([P, 1], F32)
         mean_eps = keep.tile([P, 1], F32)
-        neg_half = keep.tile([P, 1], F32)
+        rms = keep.tile([P, 1], F32)
         rstd = keep.tile([P, 1], F32)
 
         nc.vector.memset(planes_o[:].bitcast(I32), 0)
         nc.vector.memset(planes_gu[:].rearrange("p w j m -> p (w j m)").bitcast(I32), 0)
         make_identity(nc, ident[:])
-        nc.gpsimd.memset(neg_half[:], -0.5)
 
-        def load_planes_gu(w, j, quadrant):
-            nc.sync.dma_start(
-                out=planes_gu[32 * quadrant : 32 * quadrant + 4 * SHARED, w, j, :].bitcast(I32),
-                in_=gu_scales[w][SHARED * j : SHARED * (j + 1), 4 * quadrant : 4 * quadrant + 4, :].bitcast(I32),
-            )
+        for w in range(2):
+            for q in range(4 * QUADRANTS):
+                first = 32 * (q // 4) + q % 4
+                nc.gpsimd.dma_start(
+                    out=planes_gu[first : first + 4 * SHARED : 4, w, :, :].bitcast(F32),
+                    in_=gu_scales[w].rearrange("(j i) q m -> q i j m", i=SHARED)[q].bitcast(F32),
+                )
 
         def load_group(g):
             pair = ring.tile([P, 2, M], U32, align_bytes=64)
@@ -115,8 +116,6 @@ def tile_transformerblocktpu_pb_k_kernel(
                     out=pair[:, w, :].bitcast(I32),
                     in_=gu_words[w][g].rearrange("p n t -> p (n t)").bitcast(I32),
                 )
-                if g // SHARED + 1 < H_GROUPS // SHARED:
-                    load_planes_gu(w, g // SHARED + 1, g % QUADRANTS)
             return pair
 
         with tc.tile_pool(name="stage1", bufs=1) as stage1, tc.tile_pool(name="junk", bufs=4) as junk_pool:
@@ -142,8 +141,6 @@ def tile_transformerblocktpu_pb_k_kernel(
                     .bitcast(I32),
                 )
                 o_words.append(chunk)
-                for w in range(2):
-                    load_planes_gu(w, 0, c)
             gu_tiles = {}
             for g in range(RING):
                 gu_tiles[g] = load_group(g)
@@ -202,7 +199,8 @@ def tile_transformerblocktpu_pb_k_kernel(
         nc.vector.tensor_scalar(
             out=mean_eps[:], in0=total[:], scalar1=1.0 / D, scalar2=EPS, op0=ALU.mult, op1=ALU.add
         )
-        nc.gpsimd.tensor_tensor(out=rstd[:], in0=mean_eps[:], in1=neg_half[:], op=ALU.pow)
+        nc.scalar.activation(out=rms[:], in_=mean_eps[:], func=ACT.Sqrt)
+        nc.vector.reciprocal(out=rstd[:], in_=rms[:])
 
         stage2 = ctx.enter_context(tc.tile_pool(name="stage2", bufs=2))
         last = ctx.enter_context(tc.tile_pool(name="last", bufs=1))

@@ -89,25 +89,24 @@ def tile_transformerblocktpu_pb_k_kernel(
         x_mid = keep.tile([P, D], F32)
         gain_all = keep.tile([P, D], BF16)
         ident = keep.tile([P, P], BF16)
-        planes_o = keep.tile([P, D], U8, align_bytes=64)
+        planes_o = keep.tile([P, O_GROUPS, O_CHUNK], U8, align_bytes=64)
         planes_gu = keep.tile([P, 2, H_GROUPS // SHARED, M], U8, align_bytes=64)
         sumsq = keep.tile([P, D // BANK], F32)
         total = keep.tile([P, 1], F32)
         mean_eps = keep.tile([P, 1], F32)
-        rms = keep.tile([P, 1], F32)
+        neg_half = keep.tile([P, 1], F32)
         rstd = keep.tile([P, 1], F32)
 
-        nc.vector.memset(planes_o[:].bitcast(I32), 0)
+        nc.vector.memset(planes_o[:].rearrange("p g n -> p (g n)").bitcast(I32), 0)
         nc.vector.memset(planes_gu[:].rearrange("p w j m -> p (w j m)").bitcast(I32), 0)
         make_identity(nc, ident[:])
+        nc.gpsimd.memset(neg_half[:], -0.5)
 
-        for w in range(2):
-            for q in range(4 * QUADRANTS):
-                first = 32 * (q // 4) + q % 4
-                nc.gpsimd.dma_start(
-                    out=planes_gu[first : first + 4 * SHARED : 4, w, :, :].bitcast(F32),
-                    in_=gu_scales[w].rearrange("(j i) q m -> q i j m", i=SHARED)[q].bitcast(F32),
-                )
+        def load_planes_gu(w, j, quadrant):
+            nc.sync.dma_start(
+                out=planes_gu[32 * quadrant : 32 * quadrant + 4 * SHARED, w, j, :].bitcast(I32),
+                in_=gu_scales[w][SHARED * j : SHARED * (j + 1), 4 * quadrant : 4 * quadrant + 4, :].bitcast(I32),
+            )
 
         def load_group(g):
             pair = ring.tile([P, 2, M], U32, align_bytes=64)
@@ -116,21 +115,26 @@ def tile_transformerblocktpu_pb_k_kernel(
                     out=pair[:, w, :].bitcast(I32),
                     in_=gu_words[w][g].rearrange("p n t -> p (n t)").bitcast(I32),
                 )
+                if g // SHARED + 1 < H_GROUPS // SHARED:
+                    load_planes_gu(w, g // SHARED + 1, g % QUADRANTS)
             return pair
 
         with tc.tile_pool(name="stage1", bufs=1) as stage1, tc.tile_pool(name="junk", bufs=4) as junk_pool:
             attn_sb = stage1.tile([P, HH], BF16)
             nc.sync.dma_start(out=attn_sb[:], in_=attn_rows)
-            for quadrant in range(QUADRANTS):
-                nc.sync.dma_start(
-                    out=planes_o[32 * quadrant : 32 * quadrant + 4 * O_GROUPS, :].bitcast(I32),
-                    in_=w_o_scales[:, 4 * quadrant : 4 * quadrant + 4, :].bitcast(I32),
-                )
+            x_sb = stage1.tile([P, D], BF16)
+            nc.sync.dma_start(out=x_sb[:], in_=x_rows)
+            for g in range(O_GROUPS):
+                for quadrant in range(QUADRANTS):
+                    nc.sync.dma_start(
+                        out=planes_o[32 * quadrant : 32 * quadrant + 4 * SHARED, g, :].bitcast(I32),
+                        in_=w_o_scales[g, 4 * quadrant : 4 * quadrant + 4, :]
+                        .rearrange("r (c n) -> c r n", c=O_CHUNKS)
+                        .bitcast(I32),
+                    )
             gain_rows = stage1.tile([P, K_PASS], BF16)
             nc.vector.memset(gain_rows[:], 0.0)
             nc.sync.dma_start(out=gain_rows[0:H_GROUPS, :], in_=rms2_scale.rearrange("(g n) -> g n", n=K_PASS))
-            x_sb = stage1.tile([P, D], BF16)
-            nc.sync.dma_start(out=x_sb[:], in_=x_rows)
             o_words = []
             for c in range(O_CHUNKS):
                 chunk = stage1.tile([P, O_GROUPS, O_CHUNK], U32, name="o_words%d" % c, align_bytes=64)
@@ -141,6 +145,8 @@ def tile_transformerblocktpu_pb_k_kernel(
                     .bitcast(I32),
                 )
                 o_words.append(chunk)
+                for w in range(2):
+                    load_planes_gu(w, 0, c)
             gu_tiles = {}
             for g in range(RING):
                 gu_tiles[g] = load_group(g)
@@ -184,7 +190,7 @@ def tile_transformerblocktpu_pb_k_kernel(
                                 lhsT=attn_codes[:, g * P : (g + 1) * P].bitcast(FP8X4),
                                 lhsT_scale=attn_scales[:, g * P : (g + 1) * P],
                                 rhs=o_words[c][:, g, cols].bitcast(FP8X4),
-                                rhs_scale=planes_o[4 * g : P, d_cols],
+                                rhs_scale=planes_o[4 * c : P, g, cols],
                                 start=(g == 0),
                                 stop=(g == O_GROUPS - 1),
                             )
@@ -199,8 +205,7 @@ def tile_transformerblocktpu_pb_k_kernel(
         nc.vector.tensor_scalar(
             out=mean_eps[:], in0=total[:], scalar1=1.0 / D, scalar2=EPS, op0=ALU.mult, op1=ALU.add
         )
-        nc.scalar.activation(out=rms[:], in_=mean_eps[:], func=ACT.Sqrt)
-        nc.vector.reciprocal(out=rstd[:], in_=rms[:])
+        nc.gpsimd.tensor_tensor(out=rstd[:], in0=mean_eps[:], in1=neg_half[:], op=ALU.pow)
 
         stage2 = ctx.enter_context(tc.tile_pool(name="stage2", bufs=2))
         last = ctx.enter_context(tc.tile_pool(name="last", bufs=1))

@@ -94,19 +94,20 @@ def tile_transformerblocktpu_pb_k_kernel(
         sumsq = keep.tile([P, D // BANK], F32)
         total = keep.tile([P, 1], F32)
         mean_eps = keep.tile([P, 1], F32)
-        neg_half = keep.tile([P, 1], F32)
+        rms = keep.tile([P, 1], F32)
         rstd = keep.tile([P, 1], F32)
 
         nc.vector.memset(planes_o[:].rearrange("p g n -> p (g n)").bitcast(I32), 0)
         nc.vector.memset(planes_gu[:].rearrange("p w j m -> p (w j m)").bitcast(I32), 0)
         make_identity(nc, ident[:])
-        nc.gpsimd.memset(neg_half[:], -0.5)
 
-        def load_planes_gu(w, j, quadrant):
-            nc.sync.dma_start(
-                out=planes_gu[32 * quadrant : 32 * quadrant + 4 * SHARED, w, j, :].bitcast(I32),
-                in_=gu_scales[w][SHARED * j : SHARED * (j + 1), 4 * quadrant : 4 * quadrant + 4, :].bitcast(I32),
-            )
+        for j in range(H_GROUPS // SHARED):
+            for w in range(2):
+                for quadrant in range(QUADRANTS):
+                    nc.gpsimd.dma_start(
+                        out=planes_gu[32 * quadrant : 32 * quadrant + 4 * SHARED, w, j, :].bitcast(F32),
+                        in_=gu_scales[w][SHARED * j : SHARED * (j + 1), 4 * quadrant : 4 * quadrant + 4, :].bitcast(F32),
+                    )
 
         def load_group(g):
             pair = ring.tile([P, 2, M], U32, align_bytes=64)
@@ -115,8 +116,6 @@ def tile_transformerblocktpu_pb_k_kernel(
                     out=pair[:, w, :].bitcast(I32),
                     in_=gu_words[w][g].rearrange("p n t -> p (n t)").bitcast(I32),
                 )
-                if g // SHARED + 1 < H_GROUPS // SHARED:
-                    load_planes_gu(w, g // SHARED + 1, g % QUADRANTS)
             return pair
 
         with tc.tile_pool(name="stage1", bufs=1) as stage1, tc.tile_pool(name="junk", bufs=4) as junk_pool:
@@ -145,8 +144,6 @@ def tile_transformerblocktpu_pb_k_kernel(
                     .bitcast(I32),
                 )
                 o_words.append(chunk)
-                for w in range(2):
-                    load_planes_gu(w, 0, c)
             gu_tiles = {}
             for g in range(RING):
                 gu_tiles[g] = load_group(g)
@@ -205,7 +202,8 @@ def tile_transformerblocktpu_pb_k_kernel(
         nc.vector.tensor_scalar(
             out=mean_eps[:], in0=total[:], scalar1=1.0 / D, scalar2=EPS, op0=ALU.mult, op1=ALU.add
         )
-        nc.gpsimd.tensor_tensor(out=rstd[:], in0=mean_eps[:], in1=neg_half[:], op=ALU.pow)
+        nc.scalar.activation(out=rms[:], in_=mean_eps[:], func=ACT.Sqrt)
+        nc.vector.reciprocal(out=rstd[:], in_=rms[:])
 
         stage2 = ctx.enter_context(tc.tile_pool(name="stage2", bufs=2))
         last = ctx.enter_context(tc.tile_pool(name="last", bufs=1))

@@ -15,6 +15,7 @@ AXIS = mybir.AxisListType
 
 P = 128
 PACK = 4
+PAIRS = 2
 K_PASS = P * PACK
 BANK = 512
 QUADRANTS = 4
@@ -37,16 +38,21 @@ M_BLOCKS = ((0, 512), (512, 512), (1024, 256))
 FLOPS = 2 * P * (HH * D + D * 2 * M)
 
 
-def turn(nc, psum, stage, ident, sorted_rows, groups):
-    grouped = stage.tile([P, groups, P, PACK], BF16, align_bytes=64)
-    for pair in range(groups // 2):
-        turned = psum.tile([P, 2, PACK, P], BF16)
+def turn(nc, psum, stage, ident, rows, passes):
+    words = rows.bitcast(F32)
+    grouped = stage.tile([P, passes, P, PACK], BF16, align_bytes=64)
+    grouped_words = grouped[:].rearrange("p g r t -> p (g r t)").bitcast(F32)
+    for pair in range(passes // 2):
+        turned = psum.tile([P, 2, PAIRS, P], F32)
         for half in range(2):
-            for t in range(PACK):
-                nc.tensor.transpose(turned[:, half, t, :], sorted_rows[:, t, 2 * pair + half, :], ident[:])
+            first = (2 * pair + half) * P * PAIRS
+            for u in range(PAIRS):
+                nc.tensor.transpose(turned[:, half, u, :], words[:, first + u : first + P * PAIRS : PAIRS], ident[:])
         nc.scalar.copy(
-            out=grouped[:, 2 * pair : 2 * pair + 2, :, :],
-            in_=turned[:].rearrange("p g t r -> p g r t"),
+            out=grouped_words[:, 2 * pair * P * PAIRS : 2 * (pair + 1) * P * PAIRS].rearrange(
+                "p (g r u) -> p g r u", g=2, u=PAIRS
+            ),
+            in_=turned[:].rearrange("p g u r -> p g r u"),
         )
     return grouped
 
@@ -88,7 +94,9 @@ def tile_transformerblocktpu_pb_k_kernel(
 
         x_mid = keep.tile([P, D], F32)
         gain_all = keep.tile([P, D], BF16)
-        ident = keep.tile([P, P], BF16)
+        gain_rows = keep.tile([P, K_PASS], BF16)
+        ident = keep.tile([P, P], F32)
+        ident_bf16 = keep.tile([P, P], BF16)
         planes_o = keep.tile([P, O_GROUPS, O_CHUNK], U8, align_bytes=64)
         planes_gu = keep.tile([P, 2, H_GROUPS // SHARED, M], U8, align_bytes=64)
         sumsq = keep.tile([P, D // BANK], F32)
@@ -97,9 +105,13 @@ def tile_transformerblocktpu_pb_k_kernel(
         rms = keep.tile([P, 1], F32)
         rstd = keep.tile([P, 1], F32)
 
-        nc.vector.memset(planes_o[:].rearrange("p g n -> p (g n)").bitcast(I32), 0)
-        nc.vector.memset(planes_gu[:].rearrange("p w j m -> p (w j m)").bitcast(I32), 0)
+        for g in range(O_GROUPS):
+            nc.vector.memset(planes_o[:, g, :].bitcast(I32), 0)
+        for w in range(2):
+            nc.vector.memset(planes_gu[:, w, :, :].rearrange("p j m -> p (j m)").bitcast(I32), 0)
+        nc.gpsimd.memset(gain_rows[:], 0.0)
         make_identity(nc, ident[:])
+        nc.vector.tensor_copy(out=ident_bf16[:], in_=ident[:])
 
         for j in range(H_GROUPS // SHARED):
             for w in range(2):
@@ -121,19 +133,18 @@ def tile_transformerblocktpu_pb_k_kernel(
         with tc.tile_pool(name="stage1", bufs=1) as stage1, tc.tile_pool(name="junk", bufs=4) as junk_pool:
             attn_sb = stage1.tile([P, HH], BF16)
             nc.sync.dma_start(out=attn_sb[:], in_=attn_rows)
+            nc.sync.dma_start(out=gain_rows[0:H_GROUPS, :], in_=rms2_scale.rearrange("(g n) -> g n", n=K_PASS))
             x_sb = stage1.tile([P, D], BF16)
-            nc.sync.dma_start(out=x_sb[:], in_=x_rows)
             for g in range(O_GROUPS):
                 for quadrant in range(QUADRANTS):
+                    if (g, quadrant) == (1, 1):
+                        nc.sync.dma_start(out=x_sb[:], in_=x_rows)
                     nc.sync.dma_start(
                         out=planes_o[32 * quadrant : 32 * quadrant + 4 * SHARED, g, :].bitcast(I32),
                         in_=w_o_scales[g, 4 * quadrant : 4 * quadrant + 4, :]
                         .rearrange("r (c n) -> c r n", c=O_CHUNKS)
                         .bitcast(I32),
                     )
-            gain_rows = stage1.tile([P, K_PASS], BF16)
-            nc.vector.memset(gain_rows[:], 0.0)
-            nc.sync.dma_start(out=gain_rows[0:H_GROUPS, :], in_=rms2_scale.rearrange("(g n) -> g n", n=K_PASS))
             o_words = []
             for c in range(O_CHUNKS):
                 chunk = stage1.tile([P, O_GROUPS, O_CHUNK], U32, name="o_words%d" % c, align_bytes=64)
@@ -151,11 +162,7 @@ def tile_transformerblocktpu_pb_k_kernel(
             with tc.psum_pool(name="psum_turn1", bufs=1) as psum_turn1, tc.psum_pool(
                 name="psum_spread", bufs=2
             ) as psum_spread, tc.psum_pool(name="psum_o", bufs=4) as psum_o:
-                attn_sorted = stage1.tile([P, PACK, O_GROUPS, P], BF16)
-                nc.vector.tensor_copy(
-                    out=attn_sorted[:], in_=attn_sb[:].rearrange("s (g p t) -> s t g p", p=P, t=PACK)
-                )
-                attn_grouped = turn(nc, psum_turn1, stage1, ident, attn_sorted, O_GROUPS)
+                attn_grouped = turn(nc, psum_turn1, stage1, ident, attn_sb[:], O_GROUPS)
                 attn_codes = stage1.tile([P, O_GROUPS * P], U32, align_bytes=64)
                 attn_scales = stage1.tile([P, O_GROUPS * P], U8, align_bytes=64)
                 quantise(nc, attn_grouped, attn_codes[:], attn_scales[:])
@@ -166,7 +173,7 @@ def tile_transformerblocktpu_pb_k_kernel(
                         g = 2 * pair + half
                         nc.tensor.matmul(
                             out=spread[:, half, :],
-                            lhsT=ident[:, g : g + 1].to_broadcast([P, P]),
+                            lhsT=ident_bf16[:, g : g + 1].to_broadcast([P, P]),
                             rhs=gain_rows[:],
                             start=True,
                             stop=True,
@@ -218,20 +225,17 @@ def tile_transformerblocktpu_pb_k_kernel(
         ]
 
         def normalise(r):
-            h_sorted = stage2.tile([P, PACK, ROUND_GROUPS, P], BF16)
+            h_rows = stage2.tile([P, ROUND_GROUPS * K_PASS], BF16)
             k_cols = slice(r * ROUND_GROUPS * K_PASS, (r + 1) * ROUND_GROUPS * K_PASS)
-            x_view = x_mid[:, k_cols].rearrange("s (g p t) -> s t g p", p=P, t=PACK)
-            gain_view = gain_all[:, k_cols].rearrange("s (g p t) -> s t g p", p=P, t=PACK)
-            for t in range(PACK):
-                nc.vector.scalar_tensor_tensor(
-                    out=h_sorted[:, t, :, :],
-                    in0=x_view[:, t],
-                    scalar=rstd[:, 0:1],
-                    in1=gain_view[:, t],
-                    op0=ALU.mult,
-                    op1=ALU.mult,
-                )
-            return h_sorted
+            nc.vector.scalar_tensor_tensor(
+                out=h_rows[:],
+                in0=x_mid[:, k_cols],
+                scalar=rstd[:, 0:1],
+                in1=gain_all[:, k_cols],
+                op0=ALU.mult,
+                op1=ALU.mult,
+            )
+            return h_rows[:]
 
         def multiply(g):
             for w in range(2):

@@ -32,7 +32,8 @@ O_CHUNKS = D // O_CHUNK
 ROUND_GROUPS = 4
 ROUNDS = H_GROUPS // ROUND_GROUPS
 SHARED = 4
-RING = 7
+RING = 8
+LATE = 5
 M_BLOCKS = ((0, 512), (512, 512), (1024, 256))
 
 FLOPS = 2 * P * (HH * D + D * 2 * M)
@@ -121,8 +122,8 @@ def tile_transformerblocktpu_pb_k_kernel(
                         in_=gu_scales[w][SHARED * j : SHARED * (j + 1), 4 * quadrant : 4 * quadrant + 4, :].bitcast(F32),
                     )
 
-        def load_group(g):
-            pair = ring.tile([P, 2, M], U32, align_bytes=64)
+        def load_group(g, pool):
+            pair = pool.tile([P, 2, M], U32, align_bytes=64)
             for w in range(2):
                 nc.sync.dma_start(
                     out=pair[:, w, :].bitcast(I32),
@@ -157,7 +158,7 @@ def tile_transformerblocktpu_pb_k_kernel(
                 o_words.append(chunk)
             gu_tiles = {}
             for g in range(RING):
-                gu_tiles[g] = load_group(g)
+                gu_tiles[g] = load_group(g, ring)
 
             with tc.psum_pool(name="psum_turn1", bufs=1) as psum_turn1, tc.psum_pool(
                 name="psum_spread", bufs=2
@@ -214,6 +215,7 @@ def tile_transformerblocktpu_pb_k_kernel(
 
         stage2 = ctx.enter_context(tc.tile_pool(name="stage2", bufs=2))
         last = ctx.enter_context(tc.tile_pool(name="last", bufs=1))
+        late = ctx.enter_context(tc.tile_pool(name="late", bufs=LATE))
         psum_turn2 = ctx.enter_context(tc.psum_pool(name="psum_turn2", bufs=2))
         psum_gu = ctx.enter_context(tc.psum_pool(name="psum_gu", bufs=1))
 
@@ -223,6 +225,9 @@ def tile_transformerblocktpu_pb_k_kernel(
             [psum_gu.tile([P, width], F32, name="acc%d_%d" % (w, first)) for first, width in M_BLOCKS]
             for w in range(2)
         ]
+
+        for g in range(RING, RING + LATE):
+            gu_tiles[g] = load_group(g, late)
 
         def normalise(r):
             h_rows = stage2.tile([P, ROUND_GROUPS * K_PASS], BF16)
@@ -260,8 +265,8 @@ def tile_transformerblocktpu_pb_k_kernel(
                 quantise(nc, h_grouped[done], h_codes[:, word_cols], h_scales[:, word_cols])
                 for g in range(done * ROUND_GROUPS, (done + 1) * ROUND_GROUPS):
                     multiply(g)
-                    if g + RING < H_GROUPS:
-                        gu_tiles[g + RING] = load_group(g + RING)
+                    if g + RING + LATE < H_GROUPS:
+                        gu_tiles[g + RING + LATE] = load_group(g + RING + LATE, ring)
 
         for c in range(O_CHUNKS):
             d_cols = slice(c * O_CHUNK, (c + 1) * O_CHUNK)

@@ -27,6 +27,7 @@ EPS = 1e-6
 
 O_GROUPS = HH // K_PASS
 H_GROUPS = D // K_PASS
+O_LOAD = 4096
 O_CHUNK = 2048
 O_CHUNKS = D // O_CHUNK
 ROUND_GROUPS = 4
@@ -147,11 +148,11 @@ def tile_transformerblocktpu_pb_k_kernel(
                         .bitcast(I32),
                     )
             o_words = []
-            for c in range(O_CHUNKS):
-                chunk = stage1.tile([P, O_GROUPS, O_CHUNK], U32, name="o_words%d" % c, align_bytes=64)
+            for c in range(D // O_LOAD):
+                chunk = stage1.tile([P, O_GROUPS, O_LOAD], U32, name="o_words%d" % c, align_bytes=64)
                 nc.sync.dma_start(
                     out=chunk[:].bitcast(I32),
-                    in_=w_o_words[:, :, c * O_CHUNK : (c + 1) * O_CHUNK, :]
+                    in_=w_o_words[:, :, c * O_LOAD : (c + 1) * O_LOAD, :]
                     .rearrange("g p n t -> p g (n t)")
                     .bitcast(I32),
                 )
@@ -187,21 +188,23 @@ def tile_transformerblocktpu_pb_k_kernel(
                 for c in range(O_CHUNKS):
                     for b in range(O_CHUNK // BANK):
                         cols = slice(b * BANK, (b + 1) * BANK)
-                        d_cols = slice(c * O_CHUNK + b * BANK, c * O_CHUNK + (b + 1) * BANK)
+                        d_first = c * O_CHUNK + b * BANK
+                        d_cols = slice(d_first, d_first + BANK)
+                        load, l_first = divmod(d_first, O_LOAD)
                         acc = psum_o.tile([P, BANK], F32)
                         for g in range(O_GROUPS):
                             nc.tensor.matmul_mx(
                                 out=acc[:],
                                 lhsT=attn_codes[:, g * P : (g + 1) * P].bitcast(FP8X4),
                                 lhsT_scale=attn_scales[:, g * P : (g + 1) * P],
-                                rhs=o_words[c][:, g, cols].bitcast(FP8X4),
+                                rhs=o_words[load][:, g, l_first : l_first + BANK].bitcast(FP8X4),
                                 rhs_scale=planes_o[4 * c : P, g, cols],
                                 start=(g == 0),
                                 stop=(g == O_GROUPS - 1),
                             )
                         nc.vector.tensor_tensor(out=x_mid[:, d_cols], in0=acc[:], in1=x_sb[:, d_cols], op=ALU.add)
                         junk = junk_pool.tile([P, BANK], BF16)
-                        bank = c * (O_CHUNK // BANK) + b
+                        bank = d_first // BANK
                         nc.scalar.activation(
                             out=junk[:], in_=x_mid[:, d_cols], func=ACT.Square, accum_out=sumsq[:, bank : bank + 1]
                         )
@@ -268,9 +271,7 @@ def tile_transformerblocktpu_pb_k_kernel(
                     if g + RING + LATE < H_GROUPS:
                         gu_tiles[g + RING + LATE] = load_group(g + RING + LATE, ring)
 
-        for c in range(O_CHUNKS):
-            d_cols = slice(c * O_CHUNK, (c + 1) * O_CHUNK)
-            nc.sync.dma_start(out=x_mid_rows[:, d_cols], in_=x_mid[:, d_cols])
+        nc.sync.dma_start(out=x_mid_rows, in_=x_mid[:])
 
         gate_act = last.tile([P, M], F32)
         g_sb = last.tile([P, M], F32)

@@ -33,6 +33,7 @@ O_CHUNKS = D // O_CHUNK
 ROUND_GROUPS = 4
 ROUNDS = H_GROUPS // ROUND_GROUPS
 SHARED = 4
+AHEAD = 3
 RING = 8
 LATE = 5
 M_BLOCKS = ((0, 512), (512, 512), (1024, 256))
@@ -135,20 +136,19 @@ def tile_transformerblocktpu_pb_k_kernel(
         with tc.tile_pool(name="stage1", bufs=1) as stage1, tc.tile_pool(name="junk", bufs=4) as junk_pool:
             attn_sb = stage1.tile([P, HH], BF16)
             nc.sync.dma_start(out=attn_sb[:], in_=attn_rows)
-            nc.sync.dma_start(out=gain_rows[0:H_GROUPS, :], in_=rms2_scale.rearrange("(g n) -> g n", n=K_PASS))
             x_sb = stage1.tile([P, D], BF16)
-            for g in range(O_GROUPS):
-                for quadrant in range(QUADRANTS):
-                    if (g, quadrant) == (1, 1):
-                        nc.sync.dma_start(out=x_sb[:], in_=x_rows)
+            nc.sync.dma_start(out=x_sb[:], in_=x_rows)
+            nc.sync.dma_start(out=gain_rows[0:H_GROUPS, :], in_=rms2_scale.rearrange("(g n) -> g n", n=K_PASS))
+            o_scale_units = [(g, quadrant) for g in range(O_GROUPS) for quadrant in range(QUADRANTS)]
+            o_words = []
+            for c in range(D // O_LOAD):
+                for g, quadrant in o_scale_units[:AHEAD] if c == 0 else o_scale_units[AHEAD:]:
                     nc.sync.dma_start(
                         out=planes_o[32 * quadrant : 32 * quadrant + 4 * SHARED, g, :].bitcast(I32),
                         in_=w_o_scales[g, 4 * quadrant : 4 * quadrant + 4, :]
                         .rearrange("r (c n) -> c r n", c=O_CHUNKS)
                         .bitcast(I32),
                     )
-            o_words = []
-            for c in range(D // O_LOAD):
                 chunk = stage1.tile([P, O_GROUPS, O_LOAD], U32, name="o_words%d" % c, align_bytes=64)
                 nc.sync.dma_start(
                     out=chunk[:].bitcast(I32),

@@ -33,6 +33,7 @@ O_CHUNKS = D // O_CHUNK
 ROUND_GROUPS = 4
 ROUNDS = H_GROUPS // ROUND_GROUPS
 SHARED = 4
+DMA_ALIGN = 256
 AHEAD = 3
 RING = 8
 LATE = 5
@@ -95,13 +96,13 @@ def tile_transformerblocktpu_pb_k_kernel(
         keep = ctx.enter_context(tc.tile_pool(name="keep", bufs=1))
         ring = ctx.enter_context(tc.tile_pool(name="ring", bufs=RING))
 
-        x_mid = keep.tile([P, D], F32)
+        x_mid = keep.tile([P, D], F32, align_bytes=DMA_ALIGN)
         gain_all = keep.tile([P, D], BF16)
         gain_rows = keep.tile([P, K_PASS], BF16)
         ident = keep.tile([P, P], F32)
         ident_bf16 = keep.tile([P, P], BF16)
-        planes_o = keep.tile([P, O_GROUPS, O_CHUNK], U8, align_bytes=64)
-        planes_gu = keep.tile([P, 2, H_GROUPS // SHARED, M], U8, align_bytes=64)
+        planes_o = keep.tile([P, O_GROUPS, O_CHUNK], U8, align_bytes=DMA_ALIGN)
+        planes_gu = keep.tile([P, 2, H_GROUPS // SHARED, M], U8, align_bytes=DMA_ALIGN)
         sumsq = keep.tile([P, D // BANK], F32)
         total = keep.tile([P, 1], F32)
         mean_eps = keep.tile([P, 1], F32)
@@ -125,7 +126,7 @@ def tile_transformerblocktpu_pb_k_kernel(
                     )
 
         def load_group(g, pool):
-            pair = pool.tile([P, 2, M], U32, align_bytes=64)
+            pair = pool.tile([P, 2, M], U32, align_bytes=DMA_ALIGN)
             for w in range(2):
                 nc.sync.dma_start(
                     out=pair[:, w, :].bitcast(I32),
@@ -134,9 +135,9 @@ def tile_transformerblocktpu_pb_k_kernel(
             return pair
 
         with tc.tile_pool(name="stage1", bufs=1) as stage1, tc.tile_pool(name="junk", bufs=4) as junk_pool:
-            attn_sb = stage1.tile([P, HH], BF16)
+            attn_sb = stage1.tile([P, HH], BF16, align_bytes=DMA_ALIGN)
             nc.sync.dma_start(out=attn_sb[:], in_=attn_rows)
-            x_sb = stage1.tile([P, D], BF16)
+            x_sb = stage1.tile([P, D], BF16, align_bytes=DMA_ALIGN)
             nc.sync.dma_start(out=x_sb[:], in_=x_rows)
             nc.sync.dma_start(out=gain_rows[0:H_GROUPS, :], in_=rms2_scale.rearrange("(g n) -> g n", n=K_PASS))
             o_scale_units = [(g, quadrant) for g in range(O_GROUPS) for quadrant in range(QUADRANTS)]
@@ -149,7 +150,7 @@ def tile_transformerblocktpu_pb_k_kernel(
                         .rearrange("r (c n) -> c r n", c=O_CHUNKS)
                         .bitcast(I32),
                     )
-                chunk = stage1.tile([P, O_GROUPS, O_LOAD], U32, name="o_words%d" % c, align_bytes=64)
+                chunk = stage1.tile([P, O_GROUPS, O_LOAD], U32, name="o_words%d" % c, align_bytes=DMA_ALIGN)
                 nc.sync.dma_start(
                     out=chunk[:].bitcast(I32),
                     in_=w_o_words[:, :, c * O_LOAD : (c + 1) * O_LOAD, :]
@@ -274,7 +275,7 @@ def tile_transformerblocktpu_pb_k_kernel(
         nc.sync.dma_start(out=x_mid_rows, in_=x_mid[:])
 
         gate_act = last.tile([P, M], F32)
-        g_sb = last.tile([P, M], F32)
+        g_sb = last.tile([P, M], F32, align_bytes=DMA_ALIGN)
         for blk, (first, width) in enumerate(M_BLOCKS):
             m_cols = slice(first, first + width)
             nc.scalar.activation(out=gate_act[:, m_cols], in_=acc_gu[0][blk][:], func=ACT.Silu)

from contextlib import ExitStack

import concourse.mybir as mybir
from concourse.masks import make_identity

F32 = mybir.dt.float32
BF16 = mybir.dt.bfloat16
I32 = mybir.dt.int32
U32 = mybir.dt.uint32
U8 = mybir.dt.uint8
FP8X4 = mybir.dt.float8_e4m3fn_x4
ALU = mybir.AluOpType
ACT = mybir.ActivationFunctionType
AXIS = mybir.AxisListType

P = 128
PACK = 4
PAIRS = 2
K_PASS = P * PACK
BANK = 512
QUADRANTS = 4

HH = 1024
D = 8192
M = 1280
EPS = 1e-6

O_GROUPS = HH // K_PASS
H_GROUPS = D // K_PASS
O_LOAD = 4096
O_CHUNK = 2048
O_CHUNKS = D // O_CHUNK
ROUND_GROUPS = 4
ROUNDS = H_GROUPS // ROUND_GROUPS
SHARED = 4
DMA_ALIGN = 256
AHEAD = 3
RING = 8
LATE = 5
M_BLOCKS = ((0, 512), (512, 512), (1024, 256))

FLOPS = 2 * P * (HH * D + D * 2 * M)


def turn(nc, psum, stage, ident, rows, passes):
    words = rows.bitcast(F32)
    grouped = stage.tile([P, passes, P, PACK], BF16, align_bytes=64)
    grouped_words = grouped[:].rearrange("p g r t -> p (g r t)").bitcast(F32)
    for pair in range(passes // 2):
        turned = psum.tile([P, 2, PAIRS, P], F32)
        for half in range(2):
            first = (2 * pair + half) * P * PAIRS
            for u in range(PAIRS):
                nc.tensor.transpose(turned[:, half, u, :], words[:, first + u : first + P * PAIRS : PAIRS], ident[:])
        nc.scalar.copy(
            out=grouped_words[:, 2 * pair * P * PAIRS : 2 * (pair + 1) * P * PAIRS].rearrange(
                "p (g r u) -> p g r u", g=2, u=PAIRS
            ),
            in_=turned[:].rearrange("p g u r -> p g r u"),
        )
    return grouped


def quantise(nc, grouped, codes, scales):
    nc.vector.quantize_mx(
        out=codes.bitcast(FP8X4),
        scales=scales,
        in_=grouped[:].rearrange("p g r t -> p (g r t)"),
    )


def tile_transformerblocktpu_pb_k_kernel(
    tc,
    attn,
    x,
    w_o_words,
    w_o_scales,
    rms2_scale,
    w_gate_words,
    w_gate_scales,
    w_up_words,
    w_up_scales,
    out_0,
    out_1,
):
    nc = tc.nc
    attn_rows = attn.rearrange("b s k -> (b s) k")
    x_rows = x.rearrange("b s d -> (b s) d")
    x_mid_rows = out_0.rearrange("b s d -> (b s) d")
    g_rows = out_1.rearrange("b s m -> (b s) m")
    gu_words = (w_gate_words, w_up_words)
    gu_scales = (w_gate_scales, w_up_scales)

    with ExitStack() as ctx:
        ctx.enter_context(tc.manual_schedule())
        keep = ctx.enter_context(tc.tile_pool(name="keep", bufs=1))
        ring = ctx.enter_context(tc.tile_pool(name="ring", bufs=RING))

        x_mid = keep.tile([P, D], F32, align_bytes=DMA_ALIGN)
        gain_all = keep.tile([P, D], BF16)
        gain_rows = keep.tile([P, K_PASS], BF16)
        ident = keep.tile([P, P], F32)
        ident_bf16 = keep.tile([P, P], BF16)
        planes_o = keep.tile([P, O_GROUPS, O_CHUNK], U8, align_bytes=DMA_ALIGN)
        planes_gu = keep.tile([P, 2, H_GROUPS // SHARED, M], U8, align_bytes=DMA_ALIGN)
        sumsq = keep.tile([P, D // BANK], F32)
        total = keep.tile([P, 1], F32)
        mean_eps = keep.tile([P, 1], F32)
        rms = keep.tile([P, 1], F32)
        rstd = keep.tile([P, 1], F32)

        for g in range(O_GROUPS):
            nc.vector.memset(planes_o[:, g, :].bitcast(I32), 0)
        for w in range(2):
            nc.vector.memset(planes_gu[:, w, :, :].rearrange("p j m -> p (j m)").bitcast(I32), 0)
        nc.gpsimd.memset(gain_rows[:], 0.0)
        make_identity(nc, ident[:])
        nc.vector.tensor_copy(out=ident_bf16[:], in_=ident[:])

        for j in range(H_GROUPS // SHARED):
            for w in range(2):
                for quadrant in range(QUADRANTS):
                    nc.gpsimd.dma_start(
                        out=planes_gu[32 * quadrant : 32 * quadrant + 4 * SHARED, w, j, :].bitcast(F32),
                        in_=gu_scales[w][SHARED * j : SHARED * (j + 1), 4 * quadrant : 4 * quadrant + 4, :].bitcast(F32),
                    )

        def load_group(g, pool):
            pair = pool.tile([P, 2, M], U32, align_bytes=DMA_ALIGN)
            for w in range(2):
                nc.sync.dma_start(
                    out=pair[:, w, :].bitcast(I32),
                    in_=gu_words[w][g].rearrange("p n t -> p (n t)").bitcast(I32),
                )
            return pair

        with tc.tile_pool(name="stage1", bufs=1) as stage1, tc.tile_pool(name="junk", bufs=4) as junk_pool:
            attn_sb = stage1.tile([P, HH], BF16, align_bytes=DMA_ALIGN)
            nc.sync.dma_start(out=attn_sb[:], in_=attn_rows)
            x_sb = stage1.tile([P, D], BF16, align_bytes=DMA_ALIGN)
            nc.sync.dma_start(out=x_sb[:], in_=x_rows)
            nc.sync.dma_start(out=gain_rows[0:H_GROUPS, :], in_=rms2_scale.rearrange("(g n) -> g n", n=K_PASS))
            o_scale_units = [(g, quadrant) for g in range(O_GROUPS) for quadrant in range(QUADRANTS)]
            o_words = []
            for c in range(D // O_LOAD):
                for g, quadrant in o_scale_units[:AHEAD] if c == 0 else o_scale_units[AHEAD:]:
                    nc.sync.dma_start(
                        out=planes_o[32 * quadrant : 32 * quadrant + 4 * SHARED, g, :].bitcast(I32),
                        in_=w_o_scales[g, 4 * quadrant : 4 * quadrant + 4, :]
                        .rearrange("r (c n) -> c r n", c=O_CHUNKS)
                        .bitcast(I32),
                    )
                chunk = stage1.tile([P, O_GROUPS, O_LOAD], U32, name="o_words%d" % c, align_bytes=DMA_ALIGN)
                nc.sync.dma_start(
                    out=chunk[:].bitcast(I32),
                    in_=w_o_words[:, :, c * O_LOAD : (c + 1) * O_LOAD, :]
                    .rearrange("g p n t -> p g (n t)")
                    .bitcast(I32),
                )
                o_words.append(chunk)
            gu_tiles = {}
            for g in range(RING):
                gu_tiles[g] = load_group(g, ring)

            with tc.psum_pool(name="psum_turn1", bufs=1) as psum_turn1, tc.psum_pool(
                name="psum_spread", bufs=2
            ) as psum_spread, tc.psum_pool(name="psum_o", bufs=4) as psum_o:
                attn_grouped = turn(nc, psum_turn1, stage1, ident, attn_sb[:], O_GROUPS)
                attn_codes = stage1.tile([P, O_GROUPS * P], U32, align_bytes=64)
                attn_scales = stage1.tile([P, O_GROUPS * P], U8, align_bytes=64)
                quantise(nc, attn_grouped, attn_codes[:], attn_scales[:])

                for pair in range(H_GROUPS // 2):
                    spread = psum_spread.tile([P, 2, K_PASS], BF16)
                    for half in range(2):
                        g = 2 * pair + half
                        nc.tensor.matmul(
                            out=spread[:, half, :],
                            lhsT=ident_bf16[:, g : g + 1].to_broadcast([P, P]),
                            rhs=gain_rows[:],
                            start=True,
                            stop=True,
                        )
                    nc.scalar.copy(
                        out=gain_all[:, 2 * pair * K_PASS : 2 * (pair + 1) * K_PASS],
                        in_=spread[:].rearrange("p h n -> p (h n)"),
                    )

                for c in range(O_CHUNKS):
                    for b in range(O_CHUNK // BANK):
                        cols = slice(b * BANK, (b + 1) * BANK)
                        d_first = c * O_CHUNK + b * BANK
                        d_cols = slice(d_first, d_first + BANK)
                        load, l_first = divmod(d_first, O_LOAD)
                        acc = psum_o.tile([P, BANK], F32)
                        for g in range(O_GROUPS):
                            nc.tensor.matmul_mx(
                                out=acc[:],
                                lhsT=attn_codes[:, g * P : (g + 1) * P].bitcast(FP8X4),
                                lhsT_scale=attn_scales[:, g * P : (g + 1) * P],
                                rhs=o_words[load][:, g, l_first : l_first + BANK].bitcast(FP8X4),
                                rhs_scale=planes_o[4 * c : P, g, cols],
                                start=(g == 0),
                                stop=(g == O_GROUPS - 1),
                            )
                        nc.vector.tensor_tensor(out=x_mid[:, d_cols], in0=acc[:], in1=x_sb[:, d_cols], op=ALU.add)
                        junk = junk_pool.tile([P, BANK], BF16)
                        bank = d_first // BANK
                        nc.scalar.activation(
                            out=junk[:], in_=x_mid[:, d_cols], func=ACT.Square, accum_out=sumsq[:, bank : bank + 1]
                        )

        nc.vector.tensor_reduce(out=total[:], in_=sumsq[:], axis=AXIS.X, op=ALU.add)
        nc.vector.tensor_scalar(
            out=mean_eps[:], in0=total[:], scalar1=1.0 / D, scalar2=EPS, op0=ALU.mult, op1=ALU.add
        )
        nc.scalar.activation(out=rms[:], in_=mean_eps[:], func=ACT.Sqrt)
        nc.vector.reciprocal(out=rstd[:], in_=rms[:])

        stage2 = ctx.enter_context(tc.tile_pool(name="stage2", bufs=2))
        last = ctx.enter_context(tc.tile_pool(name="last", bufs=1))
        late = ctx.enter_context(tc.tile_pool(name="late", bufs=LATE))
        psum_turn2 = ctx.enter_context(tc.psum_pool(name="psum_turn2", bufs=2))
        psum_gu = ctx.enter_context(tc.psum_pool(name="psum_gu", bufs=1))

        h_codes = last.tile([P, H_GROUPS * P], U32, align_bytes=64)
        h_scales = last.tile([P, H_GROUPS * P], U8, align_bytes=64)
        acc_gu = [
            [psum_gu.tile([P, width], F32, name="acc%d_%d" % (w, first)) for first, width in M_BLOCKS]
            for w in range(2)
        ]

        for g in range(RING, RING + LATE):
            gu_tiles[g] = load_group(g, late)

        def normalise(r):
            h_rows = stage2.tile([P, ROUND_GROUPS * K_PASS], BF16)
            k_cols = slice(r * ROUND_GROUPS * K_PASS, (r + 1) * ROUND_GROUPS * K_PASS)
            nc.vector.scalar_tensor_tensor(
                out=h_rows[:],
                in0=x_mid[:, k_cols],
                scalar=rstd[:, 0:1],
                in1=gain_all[:, k_cols],
                op0=ALU.mult,
                op1=ALU.mult,
            )
            return h_rows[:]

        def multiply(g):
            for w in range(2):
                for blk, (first, width) in enumerate(M_BLOCKS):
                    nc.tensor.matmul_mx(
                        out=acc_gu[w][blk][:],
                        lhsT=h_codes[:, g * P : (g + 1) * P].bitcast(FP8X4),
                        lhsT_scale=h_scales[:, g * P : (g + 1) * P],
                        rhs=gu_tiles[g][:, w, first : first + width].bitcast(FP8X4),
                        rhs_scale=planes_gu[4 * (g % SHARED) : P, w, g // SHARED, first : first + width],
                        start=(g == 0),
                        stop=(g == H_GROUPS - 1),
                    )

        h_grouped = {}
        for r in range(ROUNDS + 1):
            if r < ROUNDS:
                h_grouped[r] = turn(nc, psum_turn2, stage2, ident, normalise(r), ROUND_GROUPS)
            if r > 0:
                done = r - 1
                word_cols = slice(done * ROUND_GROUPS * P, (done + 1) * ROUND_GROUPS * P)
                quantise(nc, h_grouped[done], h_codes[:, word_cols], h_scales[:, word_cols])
                for g in range(done * ROUND_GROUPS, (done + 1) * ROUND_GROUPS):
                    multiply(g)
                    if g + RING + LATE < H_GROUPS:
                        gu_tiles[g + RING + LATE] = load_group(g + RING + LATE, ring)

        nc.sync.dma_start(out=x_mid_rows, in_=x_mid[:])

        gate_act = last.tile([P, M], F32)
        g_sb = last.tile([P, M], F32, align_bytes=DMA_ALIGN)
        for blk, (first, width) in enumerate(M_BLOCKS):
            m_cols = slice(first, first + width)
            nc.scalar.activation(out=gate_act[:, m_cols], in_=acc_gu[0][blk][:], func=ACT.Silu)
            nc.vector.tensor_tensor(out=g_sb[:, m_cols], in0=acc_gu[1][blk][:], in1=gate_act[:, m_cols], op=ALU.mult)
        nc.sync.dma_start(out=g_rows, in_=g_sb[:])
